import numpy as np
import ml_dtypes


def mxq(x, axis, fmt="e4m3"):
    dtype, down = {"e4m3": (ml_dtypes.float8_e4m3fn, 7), "e5m2": (ml_dtypes.float8_e5m2, 14)}[fmt]
    v = np.moveaxis(np.asarray(x, np.float32).astype(ml_dtypes.bfloat16).astype(np.float64), axis, -1)
    blocks = v.reshape(v.shape[:-1] + (-1, 32))
    amax = np.abs(blocks).max(-1, keepdims=True)
    byte = np.maximum(np.where(amax > 0, np.frexp(amax)[1] - 1 + 127, 0) - down, 1)
    scale = np.exp2(byte - 127.0)
    codes = (blocks / scale).astype(np.float32).astype(dtype).astype(np.float64)
    return np.moveaxis((codes * scale).reshape(v.shape), -1, axis)


WIDE = False


def mx_kscale(k):
    if not WIDE:
        return np.ones(k)
    levels = np.array([30, -30])
    if k % 512:
        return np.exp2(np.random.permutation(np.resize(levels, k // 32))).repeat(32)
    a = np.empty((k // 512, 16))
    for p in range(k // 512):
        a[p, :8] = np.random.permutation(np.resize(levels, 8))
        for g in range(8):
            far = levels[np.abs(levels - a[p, g]) >= 10]
            a[p, g + 8] = far[np.random.randint(len(far))]
    return np.exp2(a.ravel()).repeat(32)


BF16 = ml_dtypes.bfloat16


def bf(x):
    return np.asarray(x, np.float32).astype(BF16)


def f64(x):
    return np.asarray(x).astype(np.float64)


B, N1, N2, D, H, E = 4, 15, 17, 1024, 16, 64
N = N1 * N2 + 1
NDIMS = 2
KMAX = E // (2 * NDIMS)
BASE = 10000.0
PMAX = 3.0


def rope2d(xh, pos0, pos1):
    theta = 1.0 / (BASE ** (np.arange(KMAX) / KMAX))
    ang0 = np.broadcast_to(pos0[:, :, None, None] * theta, (B, N1, N2, KMAX))
    ang1 = np.broadcast_to(pos1[:, None, :, None] * theta, (B, N1, N2, KMAX))
    ang = np.concatenate([ang0, ang1], axis=-1).reshape(B, N - 1, 1, E // 2)
    cos, sin = np.cos(ang), np.sin(ang)
    t = xh[:, 1:]
    tr, ti = t[..., 0::2], t[..., 1::2]
    rr = tr * cos - ti * sin
    ri = tr * sin + ti * cos
    rot = np.stack([rr, ri], axis=-1).reshape(B, N - 1, H, E)
    return np.concatenate([xh[:, :1], rot], axis=1)


def setup_inputs():
    s = mx_kscale(D)
    return {"x": bf(np.random.standard_normal((B, N, D)) * s),
            "pos0": bf(np.random.uniform(-1.0, 1.0, (B, N1)) * PMAX),
            "pos1": bf(np.random.uniform(-1.0, 1.0, (B, N2)) * PMAX),
            "wq": bf(np.random.standard_normal((H * E, D)) * 1.5 / np.sqrt(D) / s),
            "wk": bf(np.random.standard_normal((H * E, D)) * 1.5 / np.sqrt(D) / s)}


def reference(x, pos0, pos1, wq, wk):
    xq = mxq(f64(x), 2, "e5m2")
    q = (xq @ mxq(f64(wq), 1, "e4m3").T).reshape(B, N, H, E)
    k = (xq @ mxq(f64(wk), 1, "e4m3").T).reshape(B, N, H, E)
    p0, p1 = f64(pos0), f64(pos1)
    return rope2d(q, p0, p1), rope2d(k, p0, p1)

@@ -1,0 +1,368 @@
+import math
+from contextlib import ExitStack
+
+import concourse.mybir as mybir
+from concourse.masks import make_identity
+
+B, N1, N2, D, H, E = 4, 15, 17, 1024, 16, 64
+N = N1 * N2 + 1
+FLOPS = 2 * 2 * B * N * D * H * E
+
+F32 = mybir.dt.float32
+BF16 = mybir.dt.bfloat16
+I32 = mybir.dt.int32
+U32 = mybir.dt.uint32
+U8 = mybir.dt.uint8
+E4M3 = mybir.dt.float8_e4m3fn_x4
+E5M2 = mybir.dt.float8_e5m2_x4
+ALU = mybir.AluOpType
+ACT = mybir.ActivationFunctionType
+AX = mybir.AxisListType
+
+P = 128
+PASSES = 2
+TILES = B * N // P
+HALVES = N // P
+BLOCKS = 4
+PAIRS = E // 2
+BLOCK_PAIRS = PAIRS // BLOCKS
+HEADS = 2 * H
+FREQS = 16
+GRID_PAD = 18
+BANK = 512
+EARLY = 2
+HEAD = 11
+RUN = 4
+VECTOR_COPIES = (2, 4)
+VECTOR_COS = (1, 3, 5)
+
+
+def tile_attention_pa_kernel(tc, x, pos0, pos1, wq, wk, out_0, out_1):
+    nc = tc.nc
+    x_rows = x.flatten_outer_dims()
+    outs = [o.rearrange("b n h e -> (b n) (h e)") for o in (out_0, out_1)]
+    w_blocks = [
+        w.rearrange("(h n r s) k -> n h r (s k)", h=H, n=BLOCKS, r=BLOCK_PAIRS, s=2) for w in (wq, wk)
+    ]
+
+    with ExitStack() as ctx:
+        keep = ctx.enter_context(tc.tile_pool(name="keep", bufs=1))
+        stage = ctx.enter_context(tc.tile_pool(name="stage", bufs=2))
+        psum = ctx.enter_context(tc.psum_pool(name="psum", bufs=4))
+        ctx.enter_context(tc.manual_schedule())
+
+        x_raw = keep.tile([P, TILES, D], BF16)
+        w_raw = keep.tile([P, BLOCKS, 2, 2 * D], BF16)
+        x_codes = keep.tile([P, TILES, PASSES * P], U32, align_bytes=64)
+        x_scales = keep.tile([P, TILES, PASSES * P], U8, align_bytes=64)
+        w_codes = keep.tile([P, BLOCKS, PASSES, BANK], U32, align_bytes=64)
+        w_scales = keep.tile([P, BLOCKS, PASSES, BANK], U8, align_bytes=64)
+        result = keep.tile([P, TILES, HEADS, E], F32)
+
+        def load_w(n):
+            for proj in range(2):
+                nc.sync.dma_start(out=w_raw[:, n, proj, :], in_=w_blocks[proj][n])
+
+        def load_x(t0, count):
+            nc.sync.dma_start(
+                out=x_raw[:, t0 : t0 + count, :],
+                in_=x_rows[t0 * P : (t0 + count) * P, :].rearrange("(t p) k -> p t k", p=P),
+            )
+
+        pos_rows = keep.tile([P, 2, GRID_PAD], BF16)
+        nc.gpsimd.memset(pos_rows[:], 0.0)
+        load_x(0, 1)
+        nc.sync.dma_start(out=pos_rows[0:B, 0, 0:N1], in_=pos0)
+        nc.sync.dma_start(out=pos_rows[0:B, 1, 0:N2], in_=pos1)
+        load_w(0)
+        load_x(1, 1)
+        load_w(1)
+        load_w(2)
+        load_w(3)
+        load_x(2, 2)
+        load_x(4, 2)
+        load_x(6, 2)
+
+        ident = keep.tile([P, P], F32)
+        make_identity(nc, ident[:])
+        cell = keep.tile([P, HALVES, N1, N2], F32)
+        cell_flat = cell[:].rearrange("p s i j -> p (s i j)")
+        nc.gpsimd.memset(cell_flat, 0.0)
+        nc.gpsimd.affine_select(
+            out=cell_flat,
+            in_=cell_flat,
+            pattern=[[P, HALVES], [-N2, N1], [-1, N2]],
+            compare_op=ALU.not_equal,
+            fill=1.0,
+            base=-1,
+            channel_multiplier=1,
+        )
+
+        theta = keep.tile([P, FREQS], F32)
+        on_line = keep.tile([P, HALVES, 2, GRID_PAD], F32)
+        batch_pick = keep.tile([P, B], BF16)
+        nc.vector.memset(theta[:, 0:1], 1.0)
+        nc.vector.memset(on_line[:], 0.0)
+        nc.vector.tensor_scalar(
+            out=theta[:, 0:1], in0=theta[:, 0:1], scalar1=0.5 / math.pi, scalar2=None, op0=ALU.mult
+        )
+        width = 1
+        while width < FREQS:
+            nc.vector.tensor_scalar(
+                out=theta[:, width : 2 * width],
+                in0=theta[:, 0:width],
+                scalar1=10000.0 ** (-width / FREQS),
+                scalar2=None,
+                op0=ALU.mult,
+            )
+            width *= 2
+        nc.vector.tensor_copy(out=batch_pick[:], in_=ident[:, 0:B])
+        nc.vector.tensor_reduce(out=on_line[:, :, 0, 0:N1], in_=cell[:], axis=AX.X, op=ALU.add)
+        nc.vector.tensor_reduce(
+            out=on_line[:, :, 1, 0:N2], in_=cell[:].rearrange("p s i j -> p s j i"), axis=AX.X, op=ALU.add
+        )
+
+        picked = keep.tile([P, B, HALVES, 2 * GRID_PAD], F32)
+        coord = keep.tile([P, TILES * 2], F32)
+        turns = keep.tile([P, TILES * 2, FREQS], F32)
+        whole = keep.tile([P, 2, TILES * PAIRS], I32)
+        frac = keep.tile([P, 2, TILES * PAIRS], F32)
+        cos = keep.tile([P, TILES, PAIRS], F32)
+        sin = keep.tile([P, TILES, PAIRS, 2], F32)
+
+        def make_angles():
+            pos_all = psum.tile([P, B, 2 * GRID_PAD], F32, tag="flip")
+            for b in range(B):
+                nc.tensor.matmul(
+                    pos_all[:, b, :],
+                    lhsT=batch_pick[:, b : b + 1].to_broadcast([P, P]),
+                    rhs=pos_rows[:].rearrange("p a g -> p (a g)"),
+                    start=True,
+                    stop=True,
+                )
+            shape = [P, B, HALVES, 2 * GRID_PAD]
+            nc.vector.tensor_tensor(
+                out=picked[:],
+                in0=pos_all[:].unsqueeze(2).to_broadcast(shape),
+                in1=on_line[:].rearrange("p s a g -> p s (a g)").unsqueeze(1).to_broadcast(shape),
+                op=ALU.mult,
+            )
+            nc.vector.tensor_reduce(
+                out=coord[:], in_=picked[:].rearrange("p b s (a g) -> p (b s a) g", a=2), axis=AX.X, op=ALU.add
+            )
+            shape = [P, TILES * 2, FREQS]
+            nc.vector.tensor_tensor(
+                out=turns[:],
+                in0=coord[:].unsqueeze(2).to_broadcast(shape),
+                in1=theta[:].unsqueeze(1).to_broadcast(shape),
+                op=ALU.mult,
+            )
+            turns_flat = turns[:].rearrange("p c m -> p (c m)")
+            nc.vector.tensor_copy(out=whole[:, 0, :], in_=turns_flat)
+            nc.vector.tensor_scalar(out=whole[:, 1, :], in0=turns_flat, scalar1=0.25, scalar2=None, op0=ALU.add)
+            nc.vector.tensor_tensor(
+                out=frac[:],
+                in0=turns_flat.unsqueeze(1).to_broadcast([P, 2, TILES * PAIRS]),
+                in1=whole[:],
+                op=ALU.subtract,
+            )
+
+        def make_tables():
+            sin_cols = sin[:].rearrange("p t m s -> p (t m) s")
+            nc.scalar.activation(
+                out=cos[:].rearrange("p t m -> p (t m)"),
+                in_=frac[:, 1, :],
+                func=ACT.Sin,
+                scale=2 * math.pi,
+                bias=0.5 * math.pi,
+            )
+            nc.scalar.activation(out=sin_cols[:, :, 0], in_=frac[:, 0, :], func=ACT.Sin, scale=-2 * math.pi)
+            nc.scalar.activation(out=sin_cols[:, :, 1], in_=frac[:, 0, :], func=ACT.Sin, scale=2 * math.pi)
+
+        def flip_x(t):
+            words = x_raw[:, t, :].bitcast(F32)
+            bank = psum.tile([P, PASSES, 2, P], F32, tag="flip", name="flip_x")
+            for g in range(PASSES):
+                for u in range(2):
+                    nc.tensor.transpose(bank[:, g, u, :], words[:, 256 * g + u : 256 * (g + 1) : 2], ident[:])
+            return bank
+
+        def copy_out(on_vector, out, in_):
+            if on_vector:
+                nc.vector.tensor_copy(out=out, in_=in_)
+            else:
+                nc.scalar.copy(out=out, in_=in_)
+
+        def copy_x(bank, on_vector):
+            grouped = stage.tile([P, 4 * PASSES * P], BF16, tag="gx", bufs=4, align_bytes=64, name="gx")
+            copy_out(
+                on_vector,
+                grouped[:].bitcast(F32).rearrange("p (g r u) -> p g r u", g=PASSES, u=2),
+                bank[:].rearrange("p g u r -> p g r u"),
+            )
+            return grouped
+
+        def quantize_x(t, grouped):
+            nc.vector.quantize_mx(out=x_codes[:, t, :].bitcast(E5M2), scales=x_scales[:, t, :], in_=grouped[:])
+
+        def flip_w(n, g, proj):
+            words = w_raw[:, n, proj, :].bitcast(F32)
+            bank = psum.tile([P, 2, 2, P], F32, tag="flip", name="flip_w")
+            for s in range(2):
+                for u in range(2):
+                    first = 512 * s + 256 * g
+                    nc.tensor.transpose(bank[:, s, u, :], words[:, first + u : first + 256 : 2], ident[:])
+            return bank
+
+        def copy_w(bank, grouped, proj, on_vector):
+            copy_out(
+                on_vector,
+                grouped[:].bitcast(F32).rearrange("p (j c v) -> p j c v", j=2, v=4)[:, proj, :, :],
+                bank[:].rearrange("p s u c -> p c (s u)"),
+            )
+
+        def quantize_w(n, g, grouped):
+            nc.vector.quantize_mx(out=w_codes[:, n, g, :].bitcast(E4M3), scales=w_scales[:, n, g, :], in_=grouped[:])
+
+        def project(t, n):
+            acc = psum.tile([P, HEADS, BLOCK_PAIRS, 2], F32, tag="acc", name="acc")
+            for g in range(PASSES):
+                cols = slice(g * P, (g + 1) * P)
+                nc.tensor.matmul_mx(
+                    out=acc[:].rearrange("p h r s -> p (h r s)"),
+                    lhsT=x_codes[:, t, cols].bitcast(E5M2),
+                    lhsT_scale=x_scales[:, t, cols],
+                    rhs=w_codes[:, n, g, :].bitcast(E4M3),
+                    rhs_scale=w_scales[:, n, g, :],
+                    start=(g == 0),
+                    stop=(g == PASSES - 1),
+                )
+            return acc
+
+        def times_cos(t, n, acc, by_cos, on_vector):
+            first = BLOCK_PAIRS * n
+            if on_vector:
+                nc.vector.tensor_tensor(
+                    out=by_cos.rearrange("p r h s -> p r (h s)").rearrange("p r (h s) -> p r h s", s=2),
+                    in0=acc[:].rearrange("p h r s -> p r h s"),
+                    in1=cos[:, t, first : first + BLOCK_PAIRS]
+                    .unsqueeze(2)
+                    .unsqueeze(3)
+                    .to_broadcast([P, BLOCK_PAIRS, HEADS, 2]),
+                    op=ALU.mult,
+                )
+            else:
+                for r in range(BLOCK_PAIRS):
+                    nc.scalar.activation(
+                        out=by_cos[:, r, :, :],
+                        in_=acc[:, :, r, :],
+                        func=ACT.Copy,
+                        scale=cos[:, t, first + r : first + r + 1],
+                    )
+
+        def times_sin(t, n, acc, by_sin):
+            pairs = slice(BLOCK_PAIRS * n, BLOCK_PAIRS * (n + 1))
+            nc.vector.tensor_tensor(
+                out=by_sin,
+                in0=acc[:, :, :, ::-1],
+                in1=sin[:, t, pairs, :].unsqueeze(1).to_broadcast([P, HEADS, BLOCK_PAIRS, 2]),
+                op=ALU.mult,
+            )
+
+        added = [0] * TILES
+
+        def add_up(engine, t, n0, count, by_cos, by_sin):
+            slot = n0 % 2
+            feats = slice(2 * BLOCK_PAIRS * n0, 2 * BLOCK_PAIRS * (n0 + count))
+            engine.tensor_tensor(
+                out=result[:, t, :, feats].rearrange("p h (r s) -> p h r s", s=2),
+                in0=by_cos[:, slot : slot + count].rearrange("p b r h s -> p h (b r) s"),
+                in1=by_sin[:, :, slot : slot + count].rearrange("p h b r s -> p h (b r) s"),
+                op=ALU.add,
+            )
+            added[t] += count
+            if added[t] == BLOCKS:
+                for proj in range(2):
+                    nc.sync.dma_start(
+                        out=outs[proj][t * P : (t + 1) * P, :],
+                        in_=result[:, t, proj * H : (proj + 1) * H, :].rearrange("p h e -> p (h e)"),
+                    )
+
+        preps = [("x", 0, 0, 0)]
+        preps += [("w", 0, g, proj) for proj in range(2) for g in range(PASSES)]
+        preps += [("x", t, 0, 0) for t in range(1, EARLY)]
+        preps += [("w", n, g, proj) for n in range(1, BLOCKS) for proj in range(2) for g in range(PASSES)]
+        preps += [("x", t, 0, 0) for t in range(EARLY, TILES)]
+        staged = {}
+
+        def flip(index):
+            kind, which, g, proj = preps[index]
+            return flip_x(which) if kind == "x" else flip_w(which, g, proj)
+
+        def copy(index, bank):
+            kind, which, g, proj = preps[index]
+            on_vector = index in VECTOR_COPIES
+            if kind == "x":
+                return [(kind, which, g, copy_x(bank, on_vector))]
+            if proj == 0:
+                grouped = stage.tile([P, 4 * BANK], BF16, tag="gw", bufs=4, align_bytes=64, name="gw")
+                staged[(which, g)] = grouped
+            copy_w(bank, staged[(which, g)], proj, on_vector)
+            return [(kind, which, g, staged[(which, g)])] if proj == 1 else []
+
+        def quantize(jobs):
+            for kind, which, g, grouped in jobs:
+                if kind == "x":
+                    quantize_x(which, grouped)
+                else:
+                    quantize_w(which, g, grouped)
+
+        copied = []
+        for index in range(HEAD):
+            fresh = copy(index, flip(index))
+            quantize(copied)
+            copied = fresh
+            if index == 0:
+                make_angles()
+            if index == 2:
+                make_tables()
+        quantize(copied)
+
+        order = [(t, n) for n in range(BLOCKS) for t in range(EARLY)]
+        order += [(t, n) for t in range(EARLY, TILES) for n in range(BLOCKS)]
+        next_prep = HEAD
+        copied = []
+        waiting = []
+        halves = {}
+        acc_next = project(*order[0])
+        for step, (t, n) in enumerate(order):
+            acc = acc_next
+            run = list(range(next_prep, min(next_prep + RUN, len(preps)))) if step % 2 == 1 else []
+            next_prep += len(run)
+            banks = [flip(index) for index in run]
+            if step + 1 < len(order):
+                acc_next = project(*order[step + 1])
+            if n % 2 == 0:
+                by_cos = stage.tile([P, 2, BLOCK_PAIRS, HEADS, 2], F32, tag="by_cos", bufs=5, name="by_cos")
+                by_sin = stage.tile([P, HEADS, 2, BLOCK_PAIRS, 2], F32, tag="by_sin", bufs=5, name="by_sin")
+                halves[t] = (by_cos, by_sin)
+            by_cos, by_sin = halves[t]
+            times_cos(t, n, acc, by_cos[:, n % 2], step in VECTOR_COS)
+            ready = copied
+            copied = []
+            for index, bank in zip(run, banks):
+                copied += copy(index, bank)
+            quantize(ready)
+            times_sin(t, n, acc, by_sin[:, :, n % 2])
+            if t < EARLY or n == 1 or step == BLOCKS * EARLY:
+                for job in waiting:
+                    add_up(nc.vector, *job)
+                waiting = []
+            if t < EARLY:
+                waiting.append((t, n, 1, by_cos, by_sin))
+            elif n == 1:
+                add_up(nc.gpsimd, t, 0, 2, by_cos, by_sin)
+            elif n == 3:
+                waiting.append((t, 2, 2, by_cos, by_sin))
+        for job in waiting:
+            add_up(nc.vector, *job)

@@ -35,6 +35,7 @@ HEAD = 11
 RUN = 4
 VECTOR_COPIES = (2, 4)
 VECTOR_COS = (1, 3, 5)
+GPSIMD_HEADS = 12
 
 
 def tile_attention_pa_kernel(tc, x, pos0, pos1, wq, wk, out_0, out_1):
@@ -42,7 +43,7 @@ def tile_attention_pa_kernel(tc, x, pos0, pos1, wq, wk, out_0, out_1):
     x_rows = x.flatten_outer_dims()
     outs = [o.rearrange("b n h e -> (b n) (h e)") for o in (out_0, out_1)]
     w_blocks = [
-        w.rearrange("(h n r s) k -> n h r (s k)", h=H, n=BLOCKS, r=BLOCK_PAIRS, s=2) for w in (wq, wk)
+        w.rearrange("(p n s) k -> n p (s k)", n=BLOCKS, s=2) for w in (wq, wk)
     ]
 
     with ExitStack() as ctx:
@@ -240,12 +241,11 @@ def tile_attention_pa_kernel(tc, x, pos0, pos1, wq, wk, out_0, out_1):
             return acc
 
         def times_cos(t, n, acc, by_cos, on_vector):
-            first = BLOCK_PAIRS * n
             if on_vector:
                 nc.vector.tensor_tensor(
-                    out=by_cos.rearrange("p r h s -> p r (h s)").rearrange("p r (h s) -> p r h s", s=2),
+                    out=by_cos,
                     in0=acc[:].rearrange("p h r s -> p r h s"),
-                    in1=cos[:, t, first : first + BLOCK_PAIRS]
+                    in1=cos[:, t, n::BLOCKS]
                     .unsqueeze(2)
                     .unsqueeze(3)
                     .to_broadcast([P, BLOCK_PAIRS, HEADS, 2]),
@@ -257,36 +257,41 @@ def tile_attention_pa_kernel(tc, x, pos0, pos1, wq, wk, out_0, out_1):
                         out=by_cos[:, r, :, :],
                         in_=acc[:, :, r, :],
                         func=ACT.Copy,
-                        scale=cos[:, t, first + r : first + r + 1],
+                        scale=cos[:, t, BLOCKS * r + n : BLOCKS * r + n + 1],
                     )
 
         def times_sin(t, n, acc, by_sin):
-            pairs = slice(BLOCK_PAIRS * n, BLOCK_PAIRS * (n + 1))
             nc.vector.tensor_tensor(
                 out=by_sin,
                 in0=acc[:, :, :, ::-1],
-                in1=sin[:, t, pairs, :].unsqueeze(1).to_broadcast([P, HEADS, BLOCK_PAIRS, 2]),
+                in1=sin[:, t, n::BLOCKS, :].unsqueeze(1).to_broadcast([P, HEADS, BLOCK_PAIRS, 2]),
                 op=ALU.mult,
             )
 
-        added = [0] * TILES
-
-        def add_up(engine, t, n0, count, by_cos, by_sin):
-            slot = n0 % 2
-            feats = slice(2 * BLOCK_PAIRS * n0, 2 * BLOCK_PAIRS * (n0 + count))
+        def add_heads(engine, t, half, heads, by_cos, by_sin):
             engine.tensor_tensor(
-                out=result[:, t, :, feats].rearrange("p h (r s) -> p h r s", s=2),
-                in0=by_cos[:, slot : slot + count].rearrange("p b r h s -> p h (b r) s"),
-                in1=by_sin[:, :, slot : slot + count].rearrange("p h b r s -> p h (b r) s"),
+                out=result[:, t, heads, :].rearrange("p h (r c f) -> p (h r) c f", c=2, f=4)[:, :, half, :],
+                in0=by_cos[:, :, :, heads, :].rearrange("p r m h s -> p h (r m) s"),
+                in1=by_sin[:, :, heads, :, :].rearrange("p m h r s -> p (h r) m s"),
                 op=ALU.add,
             )
-            added[t] += count
-            if added[t] == BLOCKS:
+
+        def store(t, proj):
+            nc.sync.dma_start(
+                out=outs[proj][t * P : (t + 1) * P, :],
+                in_=result[:, t, proj * H : (proj + 1) * H, :].rearrange("p h e -> p (h e)"),
+            )
+
+        def add_up(t, half, first_head, by_cos, by_sin):
+            if t == TILES - 1 and half == 1:
                 for proj in range(2):
-                    nc.sync.dma_start(
-                        out=outs[proj][t * P : (t + 1) * P, :],
-                        in_=result[:, t, proj * H : (proj + 1) * H, :].rearrange("p h e -> p (h e)"),
-                    )
+                    add_heads(nc.vector, t, half, slice(proj * H, (proj + 1) * H), by_cos, by_sin)
+                    store(t, proj)
+                return
+            add_heads(nc.vector, t, half, slice(first_head, HEADS), by_cos, by_sin)
+            if half == 1:
+                for proj in range(2):
+                    store(t, proj)
 
         preps = [("x", 0, 0, 0)]
         preps += [("w", 0, g, proj) for proj in range(2) for g in range(PASSES)]
@@ -343,26 +348,25 @@ def tile_attention_pa_kernel(tc, x, pos0, pos1, wq, wk, out_0, out_1):
             if step + 1 < len(order):
                 acc_next = project(*order[step + 1])
             if n % 2 == 0:
-                by_cos = stage.tile([P, 2, BLOCK_PAIRS, HEADS, 2], F32, tag="by_cos", bufs=5, name="by_cos")
-                by_sin = stage.tile([P, HEADS, 2, BLOCK_PAIRS, 2], F32, tag="by_sin", bufs=5, name="by_sin")
+                by_cos = stage.tile([P, BLOCK_PAIRS, 2, HEADS, 2], F32, tag="by_cos", bufs=5, name="by_cos")
+                by_sin = stage.tile([P, 2, HEADS, BLOCK_PAIRS, 2], F32, tag="by_sin", bufs=5, name="by_sin")
                 halves[t] = (by_cos, by_sin)
             by_cos, by_sin = halves[t]
-            times_cos(t, n, acc, by_cos[:, n % 2], step in VECTOR_COS)
+            times_cos(t, n, acc, by_cos[:, :, n % 2], step in VECTOR_COS)
             ready = copied
             copied = []
             for index, bank in zip(run, banks):
                 copied += copy(index, bank)
             quantize(ready)
-            times_sin(t, n, acc, by_sin[:, :, n % 2])
-            if t < EARLY or n == 1 or step == BLOCKS * EARLY:
+            times_sin(t, n, acc, by_sin[:, n % 2])
+            if t < EARLY or n % 2 == 1 or step == BLOCKS * EARLY or step == len(order) - 2:
                 for job in waiting:
-                    add_up(nc.vector, *job)
+                    add_up(*job)
                 waiting = []
-            if t < EARLY:
-                waiting.append((t, n, 1, by_cos, by_sin))
-            elif n == 1:
-                add_up(nc.gpsimd, t, 0, 2, by_cos, by_sin)
-            elif n == 3:
-                waiting.append((t, 2, 2, by_cos, by_sin))
+            if n % 2 == 1:
+                shared = GPSIMD_HEADS if EARLY <= t < TILES - 1 else 0
+                if shared:
+                    add_heads(nc.gpsimd, t, n // 2, slice(0, shared), by_cos, by_sin)
+                waiting.append((t, n // 2, shared, by_cos, by_sin))
         for job in waiting:
-            add_up(nc.vector, *job)
+            add_up(*job)

@@ -30,12 +30,11 @@ HEADS = 2 * H
 FREQS = 16
 GRID_PAD = 18
 BANK = 512
-EARLY = 2
-HEAD = 11
-RUN = 4
-VECTOR_COPIES = (2, 4)
-VECTOR_COS = (1, 3, 5)
-GPSIMD_HEADS = 12
+EARLY = 7
+HEAD = 12
+RUN = 3
+VECTOR_COPIES = (3, 4, 5)
+VECTOR_COS = (0, 2, 4)
 
 
 def tile_attention_pa_kernel(tc, x, pos0, pos1, wq, wk, out_0, out_1):
@@ -76,13 +75,13 @@ def tile_attention_pa_kernel(tc, x, pos0, pos1, wq, wk, out_0, out_1):
         nc.sync.dma_start(out=pos_rows[0:B, 0, 0:N1], in_=pos0)
         nc.sync.dma_start(out=pos_rows[0:B, 1, 0:N2], in_=pos1)
         load_w(0)
-        load_x(1, 1)
         load_w(1)
-        load_w(2)
-        load_w(3)
+        load_x(1, 1)
         load_x(2, 2)
         load_x(4, 2)
         load_x(6, 2)
+        load_w(2)
+        load_w(3)
 
         ident = keep.tile([P, P], F32)
         make_identity(nc, ident[:])
@@ -282,22 +281,21 @@ def tile_attention_pa_kernel(tc, x, pos0, pos1, wq, wk, out_0, out_1):
                 in_=result[:, t, proj * H : (proj + 1) * H, :].rearrange("p h e -> p (h e)"),
             )
 
-        def add_up(t, half, first_head, by_cos, by_sin):
+        def add_up(t, half, by_cos, by_sin):
             if t == TILES - 1 and half == 1:
                 for proj in range(2):
                     add_heads(nc.vector, t, half, slice(proj * H, (proj + 1) * H), by_cos, by_sin)
                     store(t, proj)
                 return
-            add_heads(nc.vector, t, half, slice(first_head, HEADS), by_cos, by_sin)
+            add_heads(nc.vector, t, half, slice(0, HEADS), by_cos, by_sin)
             if half == 1:
                 for proj in range(2):
                     store(t, proj)
 
         preps = [("x", 0, 0, 0)]
-        preps += [("w", 0, g, proj) for proj in range(2) for g in range(PASSES)]
-        preps += [("x", t, 0, 0) for t in range(1, EARLY)]
-        preps += [("w", n, g, proj) for n in range(1, BLOCKS) for proj in range(2) for g in range(PASSES)]
-        preps += [("x", t, 0, 0) for t in range(EARLY, TILES)]
+        preps += [("w", n, g, proj) for n in (0, 1) for proj in range(2) for g in range(PASSES)]
+        preps += [("x", t, 0, 0) for t in range(1, TILES)]
+        preps += [("w", n, g, proj) for n in (2, 3) for proj in range(2) for g in range(PASSES)]
         staged = {}
 
         def flip(index):
@@ -329,11 +327,11 @@ def tile_attention_pa_kernel(tc, x, pos0, pos1, wq, wk, out_0, out_1):
             copied = fresh
             if index == 0:
                 make_angles()
-            if index == 2:
+            if index == 4:
                 make_tables()
         quantize(copied)
 
-        order = [(t, n) for n in range(BLOCKS) for t in range(EARLY)]
+        order = [(t, n) for half in range(2) for t in range(EARLY) for n in (2 * half, 2 * half + 1)]
         order += [(t, n) for t in range(EARLY, TILES) for n in range(BLOCKS)]
         next_prep = HEAD
         copied = []
@@ -342,7 +340,7 @@ def tile_attention_pa_kernel(tc, x, pos0, pos1, wq, wk, out_0, out_1):
         acc_next = project(*order[0])
         for step, (t, n) in enumerate(order):
             acc = acc_next
-            run = list(range(next_prep, min(next_prep + RUN, len(preps)))) if step % 2 == 1 else []
+            run = list(range(next_prep, min(next_prep + RUN, len(preps)))) if step % 2 == 1 and step > 1 else []
             next_prep += len(run)
             banks = [flip(index) for index in run]
             if step + 1 < len(order):
@@ -359,14 +357,8 @@ def tile_attention_pa_kernel(tc, x, pos0, pos1, wq, wk, out_0, out_1):
                 copied += copy(index, bank)
             quantize(ready)
             times_sin(t, n, acc, by_sin[:, n % 2])
-            if t < EARLY or n % 2 == 1 or step == BLOCKS * EARLY or step == len(order) - 2:
-                for job in waiting:
-                    add_up(*job)
-                waiting = []
-            if n % 2 == 1:
-                shared = GPSIMD_HEADS if EARLY <= t < TILES - 1 else 0
-                if shared:
-                    add_heads(nc.gpsimd, t, n // 2, slice(0, shared), by_cos, by_sin)
-                waiting.append((t, n // 2, shared, by_cos, by_sin))
+            for job in waiting:
+                add_up(*job)
+            waiting = [(t, n // 2, by_cos, by_sin)] if n % 2 == 1 else []
         for job in waiting:
             add_up(*job)

@@ -30,11 +30,10 @@ HEADS = 2 * H
 FREQS = 16
 GRID_PAD = 18
 BANK = 512
-EARLY = 7
-HEAD = 12
+EARLY = 5
+HEAD = 13
 RUN = 3
-VECTOR_COPIES = (3, 4, 5)
-VECTOR_COS = (0, 2, 4)
+VECTOR_COS = (0, 2, 4, 6, 9, 17, 25)
 
 
 def tile_attention_pa_kernel(tc, x, pos0, pos1, wq, wk, out_0, out_1):
@@ -59,9 +58,8 @@ def tile_attention_pa_kernel(tc, x, pos0, pos1, wq, wk, out_0, out_1):
         w_scales = keep.tile([P, BLOCKS, PASSES, BANK], U8, align_bytes=64)
         result = keep.tile([P, TILES, HEADS, E], F32)
 
-        def load_w(n):
-            for proj in range(2):
-                nc.sync.dma_start(out=w_raw[:, n, proj, :], in_=w_blocks[proj][n])
+        def load_w(n, proj):
+            nc.sync.dma_start(out=w_raw[:, n, proj, :], in_=w_blocks[proj][n])
 
         def load_x(t0, count):
             nc.sync.dma_start(
@@ -74,14 +72,13 @@ def tile_attention_pa_kernel(tc, x, pos0, pos1, wq, wk, out_0, out_1):
         load_x(0, 1)
         nc.sync.dma_start(out=pos_rows[0:B, 0, 0:N1], in_=pos0)
         nc.sync.dma_start(out=pos_rows[0:B, 1, 0:N2], in_=pos1)
-        load_w(0)
-        load_w(1)
-        load_x(1, 1)
-        load_x(2, 2)
-        load_x(4, 2)
-        load_x(6, 2)
-        load_w(2)
-        load_w(3)
+        for n in range(2):
+            for proj in range(2):
+                load_w(n, proj)
+        load_x(1, 2)
+        for late in range(4):
+            load_w(2 + late // 2, late % 2)
+            load_x(3 + late, 2 if late == 3 else 1)
 
         ident = keep.tile([P, P], F32)
         make_identity(nc, ident[:])
@@ -281,21 +278,18 @@ def tile_attention_pa_kernel(tc, x, pos0, pos1, wq, wk, out_0, out_1):
                 in_=result[:, t, proj * H : (proj + 1) * H, :].rearrange("p h e -> p (h e)"),
             )
 
-        def add_up(t, half, by_cos, by_sin):
-            if t == TILES - 1 and half == 1:
-                for proj in range(2):
-                    add_heads(nc.vector, t, half, slice(proj * H, (proj + 1) * H), by_cos, by_sin)
-                    store(t, proj)
-                return
-            add_heads(nc.vector, t, half, slice(0, HEADS), by_cos, by_sin)
+        def add_up(engine, t, half, proj, by_cos, by_sin):
+            add_heads(engine, t, half, slice(proj * H, (proj + 1) * H), by_cos, by_sin)
             if half == 1:
-                for proj in range(2):
-                    store(t, proj)
+                store(t, proj)
 
         preps = [("x", 0, 0, 0)]
         preps += [("w", n, g, proj) for n in (0, 1) for proj in range(2) for g in range(PASSES)]
-        preps += [("x", t, 0, 0) for t in range(1, TILES)]
-        preps += [("w", n, g, proj) for n in (2, 3) for proj in range(2) for g in range(PASSES)]
+        preps += [("x", 1, 0, 0)]
+        for late in range(4):
+            preps += [("x", 2 + late, 0, 0)]
+            preps += [("w", 2 + late // 2, g, late % 2) for g in range(PASSES)]
+        preps += [("x", 6, 0, 0), ("x", 7, 0, 0)]
         staged = {}
 
         def flip(index):
@@ -304,7 +298,7 @@ def tile_attention_pa_kernel(tc, x, pos0, pos1, wq, wk, out_0, out_1):
 
         def copy(index, bank):
             kind, which, g, proj = preps[index]
-            on_vector = index in VECTOR_COPIES
+            on_vector = kind == "w" and which == 1
             if kind == "x":
                 return [(kind, which, g, copy_x(bank, on_vector))]
             if proj == 0:
@@ -320,13 +314,12 @@ def tile_attention_pa_kernel(tc, x, pos0, pos1, wq, wk, out_0, out_1):
                 else:
                     quantize_w(which, g, grouped)
 
+        make_angles()
         copied = []
         for index in range(HEAD):
             fresh = copy(index, flip(index))
             quantize(copied)
             copied = fresh
-            if index == 0:
-                make_angles()
             if index == 4:
                 make_tables()
         quantize(copied)
@@ -340,7 +333,7 @@ def tile_attention_pa_kernel(tc, x, pos0, pos1, wq, wk, out_0, out_1):
         acc_next = project(*order[0])
         for step, (t, n) in enumerate(order):
             acc = acc_next
-            run = list(range(next_prep, min(next_prep + RUN, len(preps)))) if step % 2 == 1 and step > 1 else []
+            run = list(range(next_prep, min(next_prep + RUN, len(preps)))) if step % 2 == 0 and step > 0 else []
             next_prep += len(run)
             banks = [flip(index) for index in run]
             if step + 1 < len(order):
@@ -357,8 +350,15 @@ def tile_attention_pa_kernel(tc, x, pos0, pos1, wq, wk, out_0, out_1):
                 copied += copy(index, bank)
             quantize(ready)
             times_sin(t, n, acc, by_sin[:, n % 2])
-            for job in waiting:
-                add_up(*job)
-            waiting = [(t, n // 2, by_cos, by_sin)] if n % 2 == 1 else []
+            if n % 2 == 1 or step == len(order) - 2:
+                for job in waiting:
+                    add_up(nc.vector, *job)
+                waiting = []
+            if n % 2 == 1:
+                if t < TILES - 1:
+                    add_up(nc.gpsimd, t, n // 2, 0, by_cos, by_sin)
+                else:
+                    waiting.append((t, n // 2, 0, by_cos, by_sin))
+                waiting.append((t, n // 2, 1, by_cos, by_sin))
         for job in waiting:
-            add_up(*job)
+            add_up(nc.vector, *job)

@@ -6,6 +6,7 @@ from concourse.masks import make_identity
 
 B, N1, N2, D, H, E = 4, 15, 17, 1024, 16, 64
 N = N1 * N2 + 1
+BASE = 10000.0
 FLOPS = 2 * 2 * B * N * D * H * E
 
 F32 = mybir.dt.float32
@@ -17,216 +18,241 @@ E4M3 = mybir.dt.float8_e4m3fn_x4
 E5M2 = mybir.dt.float8_e5m2_x4
 ALU = mybir.AluOpType
 ACT = mybir.ActivationFunctionType
-AX = mybir.AxisListType
 
 P = 128
-PASSES = 2
-TILES = B * N // P
-HALVES = N // P
-BLOCKS = 4
-PAIRS = E // 2
-BLOCK_PAIRS = PAIRS // BLOCKS
-HEADS = 2 * H
-FREQS = 16
-GRID_PAD = 18
 BANK = 512
-EARLY = 5
-HEAD = 13
-RUN = 3
-VECTOR_COS = (0, 2, 4, 6, 9, 17, 25)
+PACK = 4
+PASSES = D // (P * PACK)
+PASS_WORDS = P * PACK // 2
+TILES = B * N // P
+PARTS = N // P
+HEADS = 2 * H
+PAIRS = E // 2
+FREQS = PAIRS // 2
+GROUPS = 4
+GROUP_PAIRS = PAIRS // GROUPS
+
+EARLY_TILES = 6
+HEAD_BANKS = 12
+RUN_BANKS = 2
+VECTOR_COS_STEPS = 8
+GPSIMD_HEADS = 12
+ROLE_BANKS = 4
+STAGED_BUFS = 4
+HALF_BUFS = 5
 
 
 def tile_attention_pa_kernel(tc, x, pos0, pos1, wq, wk, out_0, out_1):
     nc = tc.nc
     x_rows = x.flatten_outer_dims()
     outs = [o.rearrange("b n h e -> (b n) (h e)") for o in (out_0, out_1)]
-    w_blocks = [
-        w.rearrange("(p n s) k -> n p (s k)", n=BLOCKS, s=2) for w in (wq, wk)
-    ]
+    w_groups = [w.rearrange("(p n s) k -> n p (s k)", n=GROUPS, s=2) for w in (wq, wk)]
 
     with ExitStack() as ctx:
         keep = ctx.enter_context(tc.tile_pool(name="keep", bufs=1))
-        stage = ctx.enter_context(tc.tile_pool(name="stage", bufs=2))
-        psum = ctx.enter_context(tc.psum_pool(name="psum", bufs=4))
+        stage = ctx.enter_context(tc.tile_pool(name="stage", bufs=STAGED_BUFS))
+        psum = ctx.enter_context(tc.psum_pool(name="psum", bufs=ROLE_BANKS))
         ctx.enter_context(tc.manual_schedule())
 
         x_raw = keep.tile([P, TILES, D], BF16)
-        w_raw = keep.tile([P, BLOCKS, 2, 2 * D], BF16)
+        w_raw = keep.tile([P, GROUPS, 2, 2 * D], BF16)
         x_codes = keep.tile([P, TILES, PASSES * P], U32, align_bytes=64)
         x_scales = keep.tile([P, TILES, PASSES * P], U8, align_bytes=64)
-        w_codes = keep.tile([P, BLOCKS, PASSES, BANK], U32, align_bytes=64)
-        w_scales = keep.tile([P, BLOCKS, PASSES, BANK], U8, align_bytes=64)
+        w_codes = keep.tile([P, GROUPS, PASSES, BANK], U32, align_bytes=64)
+        w_scales = keep.tile([P, GROUPS, PASSES, BANK], U8, align_bytes=64)
         result = keep.tile([P, TILES, HEADS, E], F32)
 
         def load_w(n, proj):
-            nc.sync.dma_start(out=w_raw[:, n, proj, :], in_=w_blocks[proj][n])
+            nc.sync.dma_start(out=w_raw[:, n, proj, :], in_=w_groups[proj][n])
 
-        def load_x(t0, count):
+        def load_x(first, count):
             nc.sync.dma_start(
-                out=x_raw[:, t0 : t0 + count, :],
-                in_=x_rows[t0 * P : (t0 + count) * P, :].rearrange("(t p) k -> p t k", p=P),
+                out=x_raw[:, first : first + count, :],
+                in_=x_rows[first * P : (first + count) * P, :].rearrange("(t p) k -> p t k", p=P),
             )
 
-        pos_rows = keep.tile([P, 2, GRID_PAD], BF16)
-        nc.gpsimd.memset(pos_rows[:], 0.0)
+        row_pos = keep.tile([P, N1], BF16)
+        col_pos = keep.tile([P, N2], BF16)
+        nc.vector.memset(row_pos[:], 0.0)
+        nc.vector.memset(col_pos[:], 0.0)
         load_x(0, 1)
-        nc.sync.dma_start(out=pos_rows[0:B, 0, 0:N1], in_=pos0)
-        nc.sync.dma_start(out=pos_rows[0:B, 1, 0:N2], in_=pos1)
-        for n in range(2):
-            for proj in range(2):
-                load_w(n, proj)
+        nc.sync.dma_start(out=row_pos[0:B, :], in_=pos0)
+        nc.sync.dma_start(out=col_pos[0:B, :], in_=pos1)
+        early_w = [(n, proj) for n in (0, 1) for proj in range(2)]
+        late_w = [(n, proj) for n in (2, 3) for proj in range(2)]
+        for n, proj in early_w:
+            load_w(n, proj)
         load_x(1, 2)
-        for late in range(4):
-            load_w(2 + late // 2, late % 2)
-            load_x(3 + late, 2 if late == 3 else 1)
+        for index, (n, proj) in enumerate(late_w):
+            load_w(n, proj)
+            load_x(3 + index, 1 if index + 1 < len(late_w) else TILES - 3 - index)
 
         ident = keep.tile([P, P], F32)
         make_identity(nc, ident[:])
-        cell = keep.tile([P, HALVES, N1, N2], F32)
-        cell_flat = cell[:].rearrange("p s i j -> p (s i j)")
-        nc.gpsimd.memset(cell_flat, 0.0)
+        regroup = keep.tile([P, P], F32)
+        nc.gpsimd.memset(regroup[:], 0.0)
         nc.gpsimd.affine_select(
-            out=cell_flat,
-            in_=cell_flat,
-            pattern=[[P, HALVES], [-N2, N1], [-1, N2]],
+            out=regroup[:],
+            in_=regroup[:],
+            pattern=[[-1, GROUP_PAIRS], [-GROUP_PAIRS, H]],
             compare_op=ALU.not_equal,
             fill=1.0,
-            base=-1,
+            base=0,
             channel_multiplier=1,
         )
 
-        theta = keep.tile([P, FREQS], F32)
-        on_line = keep.tile([P, HALVES, 2, GRID_PAD], F32)
+        freq = keep.tile([P, FREQS], F32)
+        signs = keep.tile([P, 2], F32)
+        token_pos = keep.tile([P, 2, N], BF16)
         batch_pick = keep.tile([P, B], BF16)
-        nc.vector.memset(theta[:, 0:1], 1.0)
-        nc.vector.memset(on_line[:], 0.0)
+        nc.vector.memset(freq[:, 0:1], 1.0)
+        nc.vector.memset(token_pos[:, :, 0:1], 0.0)
+        nc.vector.memset(signs[:, 0:1], -1.0)
+        nc.vector.memset(signs[:, 1:2], 1.0)
         nc.vector.tensor_scalar(
-            out=theta[:, 0:1], in0=theta[:, 0:1], scalar1=0.5 / math.pi, scalar2=None, op0=ALU.mult
+            out=freq[:, 0:1], in0=freq[:, 0:1], scalar1=0.5 / math.pi, scalar2=None, op0=ALU.mult
         )
         width = 1
         while width < FREQS:
             nc.vector.tensor_scalar(
-                out=theta[:, width : 2 * width],
-                in0=theta[:, 0:width],
-                scalar1=10000.0 ** (-width / FREQS),
+                out=freq[:, width : 2 * width],
+                in0=freq[:, 0:width],
+                scalar1=BASE ** (-width / FREQS),
                 scalar2=None,
                 op0=ALU.mult,
             )
             width *= 2
         nc.vector.tensor_copy(out=batch_pick[:], in_=ident[:, 0:B])
-        nc.vector.tensor_reduce(out=on_line[:, :, 0, 0:N1], in_=cell[:], axis=AX.X, op=ALU.add)
-        nc.vector.tensor_reduce(
-            out=on_line[:, :, 1, 0:N2], in_=cell[:].rearrange("p s i j -> p s j i"), axis=AX.X, op=ALU.add
-        )
 
-        picked = keep.tile([P, B, HALVES, 2 * GRID_PAD], F32)
-        coord = keep.tile([P, TILES * 2], F32)
-        turns = keep.tile([P, TILES * 2, FREQS], F32)
+        turns = keep.tile([P, TILES * PAIRS], F32)
         whole = keep.tile([P, 2, TILES * PAIRS], I32)
         frac = keep.tile([P, 2, TILES * PAIRS], F32)
         cos = keep.tile([P, TILES, PAIRS], F32)
-        sin = keep.tile([P, TILES, PAIRS, 2], F32)
+        sin = keep.tile([P, TILES * PAIRS], F32)
+        signed_sin = keep.tile([P, TILES, PAIRS, 2], F32)
 
         def make_angles():
-            pos_all = psum.tile([P, B, 2 * GRID_PAD], F32, tag="flip")
-            for b in range(B):
-                nc.tensor.matmul(
-                    pos_all[:, b, :],
-                    lhsT=batch_pick[:, b : b + 1].to_broadcast([P, P]),
-                    rhs=pos_rows[:].rearrange("p a g -> p (a g)"),
-                    start=True,
-                    stop=True,
-                )
-            shape = [P, B, HALVES, 2 * GRID_PAD]
+            grid = [P, N1, N2]
+            nc.vector.tensor_copy(
+                out=token_pos[:, 0, 1:N].rearrange("p (i j) -> p i j", j=N2),
+                in_=row_pos[:].unsqueeze(2).to_broadcast(grid),
+            )
+            nc.vector.tensor_copy(
+                out=token_pos[:, 1, 1:N].rearrange("p (i j) -> p i j", j=N2),
+                in_=col_pos[:].unsqueeze(1).to_broadcast(grid),
+            )
+            coord = psum.tile([P, PARTS * 2, B], F32, tag="flip", name="coord")
+            for part in range(PARTS):
+                for axis in range(2):
+                    nc.tensor.matmul(
+                        coord[:, 2 * part + axis, :],
+                        lhsT=token_pos[:, axis, part * P : (part + 1) * P],
+                        rhs=batch_pick[:],
+                        start=True,
+                        stop=True,
+                    )
+            shape = [P, B, PARTS * 2, FREQS]
             nc.vector.tensor_tensor(
-                out=picked[:],
-                in0=pos_all[:].unsqueeze(2).to_broadcast(shape),
-                in1=on_line[:].rearrange("p s a g -> p s (a g)").unsqueeze(1).to_broadcast(shape),
+                out=turns[:].rearrange("p (b c m) -> p b c m", b=B, m=FREQS),
+                in0=coord[:].rearrange("p c b -> p b c").unsqueeze(3).to_broadcast(shape),
+                in1=freq[:].unsqueeze(1).unsqueeze(1).to_broadcast(shape),
                 op=ALU.mult,
             )
-            nc.vector.tensor_reduce(
-                out=coord[:], in_=picked[:].rearrange("p b s (a g) -> p (b s a) g", a=2), axis=AX.X, op=ALU.add
-            )
-            shape = [P, TILES * 2, FREQS]
-            nc.vector.tensor_tensor(
-                out=turns[:],
-                in0=coord[:].unsqueeze(2).to_broadcast(shape),
-                in1=theta[:].unsqueeze(1).to_broadcast(shape),
-                op=ALU.mult,
-            )
-            turns_flat = turns[:].rearrange("p c m -> p (c m)")
-            nc.vector.tensor_copy(out=whole[:, 0, :], in_=turns_flat)
-            nc.vector.tensor_scalar(out=whole[:, 1, :], in0=turns_flat, scalar1=0.25, scalar2=None, op0=ALU.add)
+            nc.vector.tensor_copy(out=whole[:, 0, :], in_=turns[:])
+            nc.vector.tensor_scalar(out=whole[:, 1, :], in0=turns[:], scalar1=0.25, scalar2=None, op0=ALU.add)
             nc.vector.tensor_tensor(
                 out=frac[:],
-                in0=turns_flat.unsqueeze(1).to_broadcast([P, 2, TILES * PAIRS]),
+                in0=turns[:].unsqueeze(1).to_broadcast([P, 2, TILES * PAIRS]),
                 in1=whole[:],
                 op=ALU.subtract,
             )
 
         def make_tables():
-            sin_cols = sin[:].rearrange("p t m s -> p (t m) s")
+            nc.scalar.activation(out=sin[:], in_=frac[:, 0, :], func=ACT.Sin, scale=2 * math.pi)
             nc.scalar.activation(
-                out=cos[:].rearrange("p t m -> p (t m)"),
+                out=cos[:].rearrange("p t j -> p (t j)"),
                 in_=frac[:, 1, :],
                 func=ACT.Sin,
                 scale=2 * math.pi,
                 bias=0.5 * math.pi,
             )
-            nc.scalar.activation(out=sin_cols[:, :, 0], in_=frac[:, 0, :], func=ACT.Sin, scale=-2 * math.pi)
-            nc.scalar.activation(out=sin_cols[:, :, 1], in_=frac[:, 0, :], func=ACT.Sin, scale=2 * math.pi)
+
+        def sign_sin():
+            shape = [P, TILES * PAIRS, 2]
+            nc.vector.tensor_tensor(
+                out=signed_sin[:].rearrange("p t j s -> p (t j) s"),
+                in0=sin[:].unsqueeze(2).to_broadcast(shape),
+                in1=signs[:].unsqueeze(1).to_broadcast(shape),
+                op=ALU.mult,
+            )
 
         def flip_x(t):
             words = x_raw[:, t, :].bitcast(F32)
             bank = psum.tile([P, PASSES, 2, P], F32, tag="flip", name="flip_x")
             for g in range(PASSES):
                 for u in range(2):
-                    nc.tensor.transpose(bank[:, g, u, :], words[:, 256 * g + u : 256 * (g + 1) : 2], ident[:])
+                    first = PASS_WORDS * g
+                    nc.tensor.transpose(bank[:, g, u, :], words[:, first + u : first + PASS_WORDS : 2], ident[:])
             return bank
 
-        def copy_out(on_vector, out, in_):
+        def flip_w(n, proj, g):
+            words = w_raw[:, n, proj, :].bitcast(F32)
+            bank = psum.tile([P, 2, 2, P], F32, tag="flip", name="flip_w")
+            for s in range(2):
+                for u in range(2):
+                    first = PASS_WORDS * (PASSES * s + g)
+                    nc.tensor.transpose(bank[:, s, u, :], words[:, first + u : first + PASS_WORDS : 2], regroup[:])
+            return bank
+
+        def copy_x(bank):
+            staged_x = stage.tile([P, PACK * PASSES * P], BF16, tag="staged_x", align_bytes=64, name="staged_x")
+            nc.scalar.copy(
+                out=staged_x[:].bitcast(F32).rearrange("p (g c u) -> p g c u", g=PASSES, u=2),
+                in_=bank[:].rearrange("p g u c -> p g c u"),
+            )
+            return staged_x
+
+        def copy_w(bank, staged_w, proj, on_vector):
+            out = staged_w[:].bitcast(F32).rearrange("p (c j v) -> p c j v", j=2, v=2 * H)[:, :, proj, :]
+            in_ = bank[:].rearrange("p s u c -> p s c u")
             if on_vector:
                 nc.vector.tensor_copy(out=out, in_=in_)
             else:
                 nc.scalar.copy(out=out, in_=in_)
 
-        def copy_x(bank, on_vector):
-            grouped = stage.tile([P, 4 * PASSES * P], BF16, tag="gx", bufs=4, align_bytes=64, name="gx")
-            copy_out(
-                on_vector,
-                grouped[:].bitcast(F32).rearrange("p (g r u) -> p g r u", g=PASSES, u=2),
-                bank[:].rearrange("p g u r -> p g r u"),
-            )
-            return grouped
+        banks_todo = [("x", 0)]
+        banks_todo += [("w", n, proj, g) for n, proj in early_w for g in range(PASSES)]
+        banks_todo += [("x", 1)]
+        for index, (n, proj) in enumerate(late_w):
+            banks_todo += [("x", 2 + index)] + [("w", n, proj, g) for g in range(PASSES)]
+        banks_todo += [("x", t) for t in range(2 + len(late_w), TILES)]
+        staged_ws = {}
 
-        def quantize_x(t, grouped):
-            nc.vector.quantize_mx(out=x_codes[:, t, :].bitcast(E5M2), scales=x_scales[:, t, :], in_=grouped[:])
+        def flip(item):
+            return flip_x(item[1]) if item[0] == "x" else flip_w(*item[1:])
 
-        def flip_w(n, g, proj):
-            words = w_raw[:, n, proj, :].bitcast(F32)
-            bank = psum.tile([P, 2, 2, P], F32, tag="flip", name="flip_w")
-            for s in range(2):
-                for u in range(2):
-                    first = 512 * s + 256 * g
-                    nc.tensor.transpose(bank[:, s, u, :], words[:, first + u : first + 256 : 2], ident[:])
-            return bank
+        def copy(item, bank):
+            if item[0] == "x":
+                t = item[1]
+                return [(x_codes[:, t, :].bitcast(E5M2), x_scales[:, t, :], copy_x(bank))]
+            n, proj, g = item[1:]
+            if proj == 0:
+                staged_ws[(n, g)] = stage.tile([P, PACK * BANK], BF16, tag="staged_w", align_bytes=64, name="staged_w")
+            copy_w(bank, staged_ws[(n, g)], proj, n == 0 and proj == 1)
+            if proj == 0:
+                return []
+            return [(w_codes[:, n, g, :].bitcast(E4M3), w_scales[:, n, g, :], staged_ws[(n, g)])]
 
-        def copy_w(bank, grouped, proj, on_vector):
-            copy_out(
-                on_vector,
-                grouped[:].bitcast(F32).rearrange("p (j c v) -> p j c v", j=2, v=4)[:, proj, :, :],
-                bank[:].rearrange("p s u c -> p c (s u)"),
-            )
-
-        def quantize_w(n, g, grouped):
-            nc.vector.quantize_mx(out=w_codes[:, n, g, :].bitcast(E4M3), scales=w_scales[:, n, g, :], in_=grouped[:])
+        def quantize(jobs):
+            for codes, scales, staged in jobs:
+                nc.vector.quantize_mx(out=codes, scales=scales, in_=staged[:])
 
         def project(t, n):
-            acc = psum.tile([P, HEADS, BLOCK_PAIRS, 2], F32, tag="acc", name="acc")
+            acc = psum.tile([P, 2, GROUP_PAIRS, HEADS], F32, tag="acc", name="acc")
             for g in range(PASSES):
                 cols = slice(g * P, (g + 1) * P)
                 nc.tensor.matmul_mx(
-                    out=acc[:].rearrange("p h r s -> p (h r s)"),
+                    out=acc[:].rearrange("p s r h -> p (s r h)"),
                     lhsT=x_codes[:, t, cols].bitcast(E5M2),
                     lhsT_scale=x_scales[:, t, cols],
                     rhs=w_codes[:, n, g, :].bitcast(E4M3),
@@ -236,31 +262,31 @@ def tile_attention_pa_kernel(tc, x, pos0, pos1, wq, wk, out_0, out_1):
                 )
             return acc
 
-        def times_cos(t, n, acc, by_cos, on_vector):
+        bank_shape = [P, GROUP_PAIRS, HEADS, 2]
+
+        def times_cos(t, n, acc, out, on_vector):
             if on_vector:
                 nc.vector.tensor_tensor(
-                    out=by_cos,
-                    in0=acc[:].rearrange("p h r s -> p r h s"),
-                    in1=cos[:, t, n::BLOCKS]
-                    .unsqueeze(2)
-                    .unsqueeze(3)
-                    .to_broadcast([P, BLOCK_PAIRS, HEADS, 2]),
+                    out=out,
+                    in0=acc[:].rearrange("p s r h -> p r h s"),
+                    in1=cos[:, t, n::GROUPS].unsqueeze(2).unsqueeze(3).to_broadcast(bank_shape),
                     op=ALU.mult,
                 )
             else:
-                for r in range(BLOCK_PAIRS):
+                for r in range(GROUP_PAIRS):
+                    pair = GROUPS * r + n
                     nc.scalar.activation(
-                        out=by_cos[:, r, :, :],
-                        in_=acc[:, :, r, :],
+                        out=out[:, r, :, :],
+                        in_=acc[:, :, r, :].rearrange("p s h -> p h s"),
                         func=ACT.Copy,
-                        scale=cos[:, t, BLOCKS * r + n : BLOCKS * r + n + 1],
+                        scale=cos[:, t, pair : pair + 1],
                     )
 
-        def times_sin(t, n, acc, by_sin):
+        def times_sin(t, n, acc, out):
             nc.vector.tensor_tensor(
-                out=by_sin,
-                in0=acc[:, :, :, ::-1],
-                in1=sin[:, t, n::BLOCKS, :].unsqueeze(1).to_broadcast([P, HEADS, BLOCK_PAIRS, 2]),
+                out=out,
+                in0=acc[:, ::-1].rearrange("p s r h -> p r h s"),
+                in1=signed_sin[:, t, n::GROUPS, :].unsqueeze(2).to_broadcast(bank_shape),
                 op=ALU.mult,
             )
 
@@ -268,7 +294,7 @@ def tile_attention_pa_kernel(tc, x, pos0, pos1, wq, wk, out_0, out_1):
             engine.tensor_tensor(
                 out=result[:, t, heads, :].rearrange("p h (r c f) -> p (h r) c f", c=2, f=4)[:, :, half, :],
                 in0=by_cos[:, :, :, heads, :].rearrange("p r m h s -> p h (r m) s"),
-                in1=by_sin[:, :, heads, :, :].rearrange("p m h r s -> p (h r) m s"),
+                in1=by_sin[:, :, :, heads, :].rearrange("p r m h s -> p h (r m) s"),
                 op=ALU.add,
             )
 
@@ -278,87 +304,63 @@ def tile_attention_pa_kernel(tc, x, pos0, pos1, wq, wk, out_0, out_1):
                 in_=result[:, t, proj * H : (proj + 1) * H, :].rearrange("p h e -> p (h e)"),
             )
 
-        def add_up(engine, t, half, proj, by_cos, by_sin):
-            add_heads(engine, t, half, slice(proj * H, (proj + 1) * H), by_cos, by_sin)
+        def finish_half(t, half, first_head, by_cos, by_sin):
+            if t == TILES - 1 and half == 1:
+                for proj in range(2):
+                    add_heads(nc.vector, t, half, slice(proj * H, (proj + 1) * H), by_cos, by_sin)
+                    store(t, proj)
+                return
+            add_heads(nc.vector, t, half, slice(first_head, HEADS), by_cos, by_sin)
             if half == 1:
-                store(t, proj)
+                for proj in range(2):
+                    store(t, proj)
 
-        preps = [("x", 0, 0, 0)]
-        preps += [("w", n, g, proj) for n in (0, 1) for proj in range(2) for g in range(PASSES)]
-        preps += [("x", 1, 0, 0)]
-        for late in range(4):
-            preps += [("x", 2 + late, 0, 0)]
-            preps += [("w", 2 + late // 2, g, late % 2) for g in range(PASSES)]
-        preps += [("x", 6, 0, 0), ("x", 7, 0, 0)]
-        staged = {}
-
-        def flip(index):
-            kind, which, g, proj = preps[index]
-            return flip_x(which) if kind == "x" else flip_w(which, g, proj)
-
-        def copy(index, bank):
-            kind, which, g, proj = preps[index]
-            on_vector = kind == "w" and which == 1
-            if kind == "x":
-                return [(kind, which, g, copy_x(bank, on_vector))]
-            if proj == 0:
-                grouped = stage.tile([P, 4 * BANK], BF16, tag="gw", bufs=4, align_bytes=64, name="gw")
-                staged[(which, g)] = grouped
-            copy_w(bank, staged[(which, g)], proj, on_vector)
-            return [(kind, which, g, staged[(which, g)])] if proj == 1 else []
-
-        def quantize(jobs):
-            for kind, which, g, grouped in jobs:
-                if kind == "x":
-                    quantize_x(which, grouped)
-                else:
-                    quantize_w(which, g, grouped)
-
-        make_angles()
+        banks_per_group = 2 * PASSES
         copied = []
-        for index in range(HEAD):
-            fresh = copy(index, flip(index))
+        for index, item in enumerate(banks_todo[:HEAD_BANKS]):
+            fresh = copy(item, flip(item))
             quantize(copied)
             copied = fresh
-            if index == 4:
+            if index == 0:
+                make_angles()
+            if index == banks_per_group:
                 make_tables()
+            if index == 2 * banks_per_group:
+                sign_sin()
         quantize(copied)
+        banks_todo = banks_todo[HEAD_BANKS:]
 
-        order = [(t, n) for half in range(2) for t in range(EARLY) for n in (2 * half, 2 * half + 1)]
-        order += [(t, n) for t in range(EARLY, TILES) for n in range(BLOCKS)]
-        next_prep = HEAD
+        steps = [(t, 2 * half + m) for half in range(2) for t in range(EARLY_TILES) for m in range(2)]
+        steps += [(t, n) for t in range(EARLY_TILES, TILES) for n in range(GROUPS)]
         copied = []
         waiting = []
-        halves = {}
-        acc_next = project(*order[0])
-        for step, (t, n) in enumerate(order):
+        acc_next = project(*steps[0])
+        for step, (t, n) in enumerate(steps):
+            half, m = divmod(n, 2)
             acc = acc_next
-            run = list(range(next_prep, min(next_prep + RUN, len(preps)))) if step % 2 == 0 and step > 0 else []
-            next_prep += len(run)
-            banks = [flip(index) for index in run]
-            if step + 1 < len(order):
-                acc_next = project(*order[step + 1])
-            if n % 2 == 0:
-                by_cos = stage.tile([P, BLOCK_PAIRS, 2, HEADS, 2], F32, tag="by_cos", bufs=5, name="by_cos")
-                by_sin = stage.tile([P, 2, HEADS, BLOCK_PAIRS, 2], F32, tag="by_sin", bufs=5, name="by_sin")
-                halves[t] = (by_cos, by_sin)
-            by_cos, by_sin = halves[t]
-            times_cos(t, n, acc, by_cos[:, :, n % 2], step in VECTOR_COS)
+            run = banks_todo[:RUN_BANKS] if m == 0 else []
+            banks_todo = banks_todo[len(run) :]
+            flipped = [flip(item) for item in run]
+            if step + 1 < len(steps):
+                acc_next = project(*steps[step + 1])
+            if m == 0:
+                by_cos = stage.tile([P, GROUP_PAIRS, 2, HEADS, 2], F32, tag="by_cos", bufs=HALF_BUFS, name="by_cos")
+                by_sin = stage.tile([P, GROUP_PAIRS, 2, HEADS, 2], F32, tag="by_sin", bufs=HALF_BUFS, name="by_sin")
+            times_cos(t, n, acc, by_cos[:, :, m], m == 0 and step < VECTOR_COS_STEPS)
             ready = copied
             copied = []
-            for index, bank in zip(run, banks):
-                copied += copy(index, bank)
+            for item, bank in zip(run, flipped):
+                copied += copy(item, bank)
             quantize(ready)
-            times_sin(t, n, acc, by_sin[:, n % 2])
-            if n % 2 == 1 or step == len(order) - 2:
+            times_sin(t, n, acc, by_sin[:, :, m])
+            if m == 1 or step == len(steps) - 2:
                 for job in waiting:
-                    add_up(nc.vector, *job)
+                    finish_half(*job)
                 waiting = []
-            if n % 2 == 1:
-                if t < TILES - 1:
-                    add_up(nc.gpsimd, t, n // 2, 0, by_cos, by_sin)
-                else:
-                    waiting.append((t, n // 2, 0, by_cos, by_sin))
-                waiting.append((t, n // 2, 1, by_cos, by_sin))
+            if m == 1:
+                shared = GPSIMD_HEADS if t < TILES - 1 else 0
+                if shared:
+                    add_heads(nc.gpsimd, t, half, slice(0, shared), by_cos, by_sin)
+                waiting.append((t, half, shared, by_cos, by_sin))
         for job in waiting:
-            add_up(nc.vector, *job)
+            finish_half(*job)

import math
from contextlib import ExitStack

import concourse.mybir as mybir
from concourse.masks import make_identity

B, N1, N2, D, H, E = 4, 15, 17, 1024, 16, 64
N = N1 * N2 + 1
BASE = 10000.0
FLOPS = 2 * 2 * B * N * D * H * E

F32 = mybir.dt.float32
BF16 = mybir.dt.bfloat16
I32 = mybir.dt.int32
U32 = mybir.dt.uint32
U8 = mybir.dt.uint8
E4M3 = mybir.dt.float8_e4m3fn_x4
E5M2 = mybir.dt.float8_e5m2_x4
ALU = mybir.AluOpType
ACT = mybir.ActivationFunctionType

P = 128
BANK = 512
PACK = 4
PASSES = D // (P * PACK)
PASS_WORDS = P * PACK // 2
TILES = B * N // P
PARTS = N // P
HEADS = 2 * H
PAIRS = E // 2
FREQS = PAIRS // 2
GROUPS = 4
GROUP_PAIRS = PAIRS // GROUPS

EARLY_TILES = 6
HEAD_BANKS = 12
RUN_BANKS = 2
VECTOR_COS_STEPS = 8
GPSIMD_HEADS = 12
ROLE_BANKS = 4
STAGED_BUFS = 4
HALF_BUFS = 5


def tile_attention_pa_kernel(tc, x, pos0, pos1, wq, wk, out_0, out_1):
    nc = tc.nc
    x_rows = x.flatten_outer_dims()
    outs = [o.rearrange("b n h e -> (b n) (h e)") for o in (out_0, out_1)]
    w_groups = [w.rearrange("(p n s) k -> n p (s k)", n=GROUPS, s=2) for w in (wq, wk)]

    with ExitStack() as ctx:
        keep = ctx.enter_context(tc.tile_pool(name="keep", bufs=1))
        stage = ctx.enter_context(tc.tile_pool(name="stage", bufs=STAGED_BUFS))
        psum = ctx.enter_context(tc.psum_pool(name="psum", bufs=ROLE_BANKS))
        ctx.enter_context(tc.manual_schedule())

        x_raw = keep.tile([P, TILES, D], BF16)
        w_raw = keep.tile([P, GROUPS, 2, 2 * D], BF16)
        x_codes = keep.tile([P, TILES, PASSES * P], U32, align_bytes=64)
        x_scales = keep.tile([P, TILES, PASSES * P], U8, align_bytes=64)
        w_codes = keep.tile([P, GROUPS, PASSES, BANK], U32, align_bytes=64)
        w_scales = keep.tile([P, GROUPS, PASSES, BANK], U8, align_bytes=64)
        result = keep.tile([P, TILES, HEADS, E], F32)

        def load_w(n, proj):
            nc.sync.dma_start(out=w_raw[:, n, proj, :], in_=w_groups[proj][n])

        def load_x(first, count):
            nc.sync.dma_start(
                out=x_raw[:, first : first + count, :],
                in_=x_rows[first * P : (first + count) * P, :].rearrange("(t p) k -> p t k", p=P),
            )

        row_pos = keep.tile([P, N1], BF16)
        col_pos = keep.tile([P, N2], BF16)
        nc.vector.memset(row_pos[:], 0.0)
        nc.vector.memset(col_pos[:], 0.0)
        load_x(0, 1)
        nc.sync.dma_start(out=row_pos[0:B, :], in_=pos0)
        nc.sync.dma_start(out=col_pos[0:B, :], in_=pos1)
        early_w = [(n, proj) for n in (0, 1) for proj in range(2)]
        late_w = [(n, proj) for n in (2, 3) for proj in range(2)]
        for n, proj in early_w:
            load_w(n, proj)
        load_x(1, 2)
        for index, (n, proj) in enumerate(late_w):
            load_w(n, proj)
            load_x(3 + index, 1 if index + 1 < len(late_w) else TILES - 3 - index)

        ident = keep.tile([P, P], F32)
        make_identity(nc, ident[:])
        regroup = keep.tile([P, P], F32)
        nc.gpsimd.memset(regroup[:], 0.0)
        nc.gpsimd.affine_select(
            out=regroup[:],
            in_=regroup[:],
            pattern=[[-1, GROUP_PAIRS], [-GROUP_PAIRS, H]],
            compare_op=ALU.not_equal,
            fill=1.0,
            base=0,
            channel_multiplier=1,
        )

        freq = keep.tile([P, FREQS], F32)
        signs = keep.tile([P, 2], F32)
        token_pos = keep.tile([P, 2, N], BF16)
        batch_pick = keep.tile([P, B], BF16)
        nc.vector.memset(freq[:, 0:1], 1.0)
        nc.vector.memset(token_pos[:, :, 0:1], 0.0)
        nc.vector.memset(signs[:, 0:1], -1.0)
        nc.vector.memset(signs[:, 1:2], 1.0)
        nc.vector.tensor_scalar(
            out=freq[:, 0:1], in0=freq[:, 0:1], scalar1=0.5 / math.pi, scalar2=None, op0=ALU.mult
        )
        width = 1
        while width < FREQS:
            nc.vector.tensor_scalar(
                out=freq[:, width : 2 * width],
                in0=freq[:, 0:width],
                scalar1=BASE ** (-width / FREQS),
                scalar2=None,
                op0=ALU.mult,
            )
            width *= 2
        nc.vector.tensor_copy(out=batch_pick[:], in_=ident[:, 0:B])

        turns = keep.tile([P, TILES * PAIRS], F32)
        whole = keep.tile([P, 2, TILES * PAIRS], I32)
        frac = keep.tile([P, 2, TILES * PAIRS], F32)
        cos = keep.tile([P, TILES, PAIRS], F32)
        sin = keep.tile([P, TILES * PAIRS], F32)
        signed_sin = keep.tile([P, TILES, PAIRS, 2], F32)

        def make_angles():
            grid = [P, N1, N2]
            nc.vector.tensor_copy(
                out=token_pos[:, 0, 1:N].rearrange("p (i j) -> p i j", j=N2),
                in_=row_pos[:].unsqueeze(2).to_broadcast(grid),
            )
            nc.vector.tensor_copy(
                out=token_pos[:, 1, 1:N].rearrange("p (i j) -> p i j", j=N2),
                in_=col_pos[:].unsqueeze(1).to_broadcast(grid),
            )
            coord = psum.tile([P, PARTS * 2, B], F32, tag="flip", name="coord")
            for part in range(PARTS):
                for axis in range(2):
                    nc.tensor.matmul(
                        coord[:, 2 * part + axis, :],
                        lhsT=token_pos[:, axis, part * P : (part + 1) * P],
                        rhs=batch_pick[:],
                        start=True,
                        stop=True,
                    )
            shape = [P, B, PARTS * 2, FREQS]
            nc.vector.tensor_tensor(
                out=turns[:].rearrange("p (b c m) -> p b c m", b=B, m=FREQS),
                in0=coord[:].rearrange("p c b -> p b c").unsqueeze(3).to_broadcast(shape),
                in1=freq[:].unsqueeze(1).unsqueeze(1).to_broadcast(shape),
                op=ALU.mult,
            )
            nc.vector.tensor_copy(out=whole[:, 0, :], in_=turns[:])
            nc.vector.tensor_scalar(out=whole[:, 1, :], in0=turns[:], scalar1=0.25, scalar2=None, op0=ALU.add)
            nc.vector.tensor_tensor(
                out=frac[:],
                in0=turns[:].unsqueeze(1).to_broadcast([P, 2, TILES * PAIRS]),
                in1=whole[:],
                op=ALU.subtract,
            )

        def make_tables():
            nc.scalar.activation(out=sin[:], in_=frac[:, 0, :], func=ACT.Sin, scale=2 * math.pi)
            nc.scalar.activation(
                out=cos[:].rearrange("p t j -> p (t j)"),
                in_=frac[:, 1, :],
                func=ACT.Sin,
                scale=2 * math.pi,
                bias=0.5 * math.pi,
            )

        def sign_sin():
            shape = [P, TILES * PAIRS, 2]
            nc.vector.tensor_tensor(
                out=signed_sin[:].rearrange("p t j s -> p (t j) s"),
                in0=sin[:].unsqueeze(2).to_broadcast(shape),
                in1=signs[:].unsqueeze(1).to_broadcast(shape),
                op=ALU.mult,
            )

        def flip_x(t):
            words = x_raw[:, t, :].bitcast(F32)
            bank = psum.tile([P, PASSES, 2, P], F32, tag="flip", name="flip_x")
            for g in range(PASSES):
                for u in range(2):
                    first = PASS_WORDS * g
                    nc.tensor.transpose(bank[:, g, u, :], words[:, first + u : first + PASS_WORDS : 2], ident[:])
            return bank

        def flip_w(n, proj, g):
            words = w_raw[:, n, proj, :].bitcast(F32)
            bank = psum.tile([P, 2, 2, P], F32, tag="flip", name="flip_w")
            for s in range(2):
                for u in range(2):
                    first = PASS_WORDS * (PASSES * s + g)
                    nc.tensor.transpose(bank[:, s, u, :], words[:, first + u : first + PASS_WORDS : 2], regroup[:])
            return bank

        def copy_x(bank):
            staged_x = stage.tile([P, PACK * PASSES * P], BF16, tag="staged_x", align_bytes=64, name="staged_x")
            nc.scalar.copy(
                out=staged_x[:].bitcast(F32).rearrange("p (g c u) -> p g c u", g=PASSES, u=2),
                in_=bank[:].rearrange("p g u c -> p g c u"),
            )
            return staged_x

        def copy_w(bank, staged_w, proj, on_vector):
            out = staged_w[:].bitcast(F32).rearrange("p (c j v) -> p c j v", j=2, v=2 * H)[:, :, proj, :]
            in_ = bank[:].rearrange("p s u c -> p s c u")
            if on_vector:
                nc.vector.tensor_copy(out=out, in_=in_)
            else:
                nc.scalar.copy(out=out, in_=in_)

        banks_todo = [("x", 0)]
        banks_todo += [("w", n, proj, g) for n, proj in early_w for g in range(PASSES)]
        banks_todo += [("x", 1)]
        for index, (n, proj) in enumerate(late_w):
            banks_todo += [("x", 2 + index)] + [("w", n, proj, g) for g in range(PASSES)]
        banks_todo += [("x", t) for t in range(2 + len(late_w), TILES)]
        staged_ws = {}

        def flip(item):
            return flip_x(item[1]) if item[0] == "x" else flip_w(*item[1:])

        def copy(item, bank):
            if item[0] == "x":
                t = item[1]
                return [(x_codes[:, t, :].bitcast(E5M2), x_scales[:, t, :], copy_x(bank))]
            n, proj, g = item[1:]
            if proj == 0:
                staged_ws[(n, g)] = stage.tile([P, PACK * BANK], BF16, tag="staged_w", align_bytes=64, name="staged_w")
            copy_w(bank, staged_ws[(n, g)], proj, n == 0 and proj == 1)
            if proj == 0:
                return []
            return [(w_codes[:, n, g, :].bitcast(E4M3), w_scales[:, n, g, :], staged_ws[(n, g)])]

        def quantize(jobs):
            for codes, scales, staged in jobs:
                nc.vector.quantize_mx(out=codes, scales=scales, in_=staged[:])

        def project(t, n):
            acc = psum.tile([P, 2, GROUP_PAIRS, HEADS], F32, tag="acc", name="acc")
            for g in range(PASSES):
                cols = slice(g * P, (g + 1) * P)
                nc.tensor.matmul_mx(
                    out=acc[:].rearrange("p s r h -> p (s r h)"),
                    lhsT=x_codes[:, t, cols].bitcast(E5M2),
                    lhsT_scale=x_scales[:, t, cols],
                    rhs=w_codes[:, n, g, :].bitcast(E4M3),
                    rhs_scale=w_scales[:, n, g, :],
                    start=(g == 0),
                    stop=(g == PASSES - 1),
                )
            return acc

        bank_shape = [P, GROUP_PAIRS, HEADS, 2]

        def times_cos(t, n, acc, out, on_vector):
            if on_vector:
                nc.vector.tensor_tensor(
                    out=out,
                    in0=acc[:].rearrange("p s r h -> p r h s"),
                    in1=cos[:, t, n::GROUPS].unsqueeze(2).unsqueeze(3).to_broadcast(bank_shape),
                    op=ALU.mult,
                )
            else:
                for r in range(GROUP_PAIRS):
                    pair = GROUPS * r + n
                    nc.scalar.activation(
                        out=out[:, r, :, :],
                        in_=acc[:, :, r, :].rearrange("p s h -> p h s"),
                        func=ACT.Copy,
                        scale=cos[:, t, pair : pair + 1],
                    )

        def times_sin(t, n, acc, out):
            nc.vector.tensor_tensor(
                out=out,
                in0=acc[:, ::-1].rearrange("p s r h -> p r h s"),
                in1=signed_sin[:, t, n::GROUPS, :].unsqueeze(2).to_broadcast(bank_shape),
                op=ALU.mult,
            )

        def add_heads(engine, t, half, heads, by_cos, by_sin):
            engine.tensor_tensor(
                out=result[:, t, heads, :].rearrange("p h (r c f) -> p (h r) c f", c=2, f=4)[:, :, half, :],
                in0=by_cos[:, :, :, heads, :].rearrange("p r m h s -> p h (r m) s"),
                in1=by_sin[:, :, :, heads, :].rearrange("p r m h s -> p h (r m) s"),
                op=ALU.add,
            )

        def store(t, proj):
            nc.sync.dma_start(
                out=outs[proj][t * P : (t + 1) * P, :],
                in_=result[:, t, proj * H : (proj + 1) * H, :].rearrange("p h e -> p (h e)"),
            )

        def finish_half(t, half, first_head, by_cos, by_sin):
            if t == TILES - 1 and half == 1:
                for proj in range(2):
                    add_heads(nc.vector, t, half, slice(proj * H, (proj + 1) * H), by_cos, by_sin)
                    store(t, proj)
                return
            add_heads(nc.vector, t, half, slice(first_head, HEADS), by_cos, by_sin)
            if half == 1:
                for proj in range(2):
                    store(t, proj)

        banks_per_group = 2 * PASSES
        copied = []
        for index, item in enumerate(banks_todo[:HEAD_BANKS]):
            fresh = copy(item, flip(item))
            quantize(copied)
            copied = fresh
            if index == 0:
                make_angles()
            if index == banks_per_group:
                make_tables()
            if index == 2 * banks_per_group:
                sign_sin()
        quantize(copied)
        banks_todo = banks_todo[HEAD_BANKS:]

        steps = [(t, 2 * half + m) for half in range(2) for t in range(EARLY_TILES) for m in range(2)]
        steps += [(t, n) for t in range(EARLY_TILES, TILES) for n in range(GROUPS)]
        copied = []
        waiting = []
        acc_next = project(*steps[0])
        for step, (t, n) in enumerate(steps):
            half, m = divmod(n, 2)
            acc = acc_next
            run = banks_todo[:RUN_BANKS] if m == 0 else []
            banks_todo = banks_todo[len(run) :]
            flipped = [flip(item) for item in run]
            if step + 1 < len(steps):
                acc_next = project(*steps[step + 1])
            if m == 0:
                by_cos = stage.tile([P, GROUP_PAIRS, 2, HEADS, 2], F32, tag="by_cos", bufs=HALF_BUFS, name="by_cos")
                by_sin = stage.tile([P, GROUP_PAIRS, 2, HEADS, 2], F32, tag="by_sin", bufs=HALF_BUFS, name="by_sin")
            times_cos(t, n, acc, by_cos[:, :, m], m == 0 and step < VECTOR_COS_STEPS)
            ready = copied
            copied = []
            for item, bank in zip(run, flipped):
                copied += copy(item, bank)
            quantize(ready)
            times_sin(t, n, acc, by_sin[:, :, m])
            if m == 1 or step == len(steps) - 2:
                for job in waiting:
                    finish_half(*job)
                waiting = []
            if m == 1:
                shared = GPSIMD_HEADS if t < TILES - 1 else 0
                if shared:
                    add_heads(nc.gpsimd, t, half, slice(0, shared), by_cos, by_sin)
                waiting.append((t, half, shared, by_cos, by_sin))
        for job in waiting:
            finish_half(*job)
